import numpy as np
import ml_dtypes


def mxq(x, axis, fmt="e4m3"):
    dtype, down = {"e4m3": (ml_dtypes.float8_e4m3fn, 7), "e5m2": (ml_dtypes.float8_e5m2, 14)}[fmt]
    v = np.moveaxis(np.asarray(x, np.float32).astype(ml_dtypes.bfloat16).astype(np.float64), axis, -1)
    blocks = v.reshape(v.shape[:-1] + (-1, 32))
    amax = np.abs(blocks).max(-1, keepdims=True)
    byte = np.maximum(np.where(amax > 0, np.frexp(amax)[1] - 1 + 127, 0) - down, 1)
    scale = np.exp2(byte - 127.0)
    codes = (blocks / scale).astype(np.float32).astype(dtype).astype(np.float64)
    return np.moveaxis((codes * scale).reshape(v.shape), -1, axis)


WIDE = False


def mx_kscale(k):
    if not WIDE:
        return np.ones(k)
    levels = np.array([10, -10, 5, -5, 0])
    a = np.random.permutation(np.resize(levels, k // 512 * 4)).reshape(k // 512, 4)
    idx = np.arange(k)
    return np.exp2(a[idx // 512, idx % 128 // 32])


BF16 = ml_dtypes.bfloat16


def bf(x):
    return np.asarray(x, np.float32).astype(BF16)


def f64(x):
    return np.asarray(x).astype(np.float64)


E2M1 = np.array([0.0, 0.5, 1.0, 1.5, 2.0, 3.0, 4.0, 6.0, -0.0, -0.5, -1.0, -1.5, -2.0, -3.0, -4.0, -6.0])


def pack_weight(w, fmt):
    k, n = w.shape
    w = f64(bf(w)).reshape(k // 32, 32, n)
    amax = np.abs(w).max(1)
    if fmt == "e4m3":
        byte = np.frexp(amax)[1] - 1 + 127 - 7
    else:
        mant, ex = np.frexp(amax / 6.0)
        byte = np.where(mant > 0.5, ex, ex - 1) + 127
    byte = np.clip(np.where(amax > 0, byte, 1), 1, 254)
    scaled = (w * np.exp2(127.0 - byte)[:, None, :]).reshape(k, n).astype(np.float32)
    by_word = np.ascontiguousarray(scaled.reshape(k // 512, 128, 4, n).transpose(0, 1, 3, 2))
    if fmt == "e4m3":
        words = by_word.astype(ml_dtypes.float8_e4m3fn).view(np.uint8)
    else:
        c = by_word.astype(ml_dtypes.float4_e2m1fn).view(np.uint8) & 0xF
        words = c[..., 0::2] | (c[..., 1::2] << 4)
    return np.ascontiguousarray(words), np.ascontiguousarray(byte.astype(np.uint8).reshape(k // 512, 16, n))


def unpack_weight(words, scales, fmt):
    g, p, n, _ = words.shape
    if fmt == "e4m3":
        vals = np.ascontiguousarray(words).view(ml_dtypes.float8_e4m3fn).astype(np.float64)
    else:
        nib = np.empty((g, p, n, 4), np.uint8)
        nib[..., 0::2] = words & 0xF
        nib[..., 1::2] = words >> 4
        vals = E2M1[nib]
    vals = vals * np.repeat(np.exp2(scales.astype(np.float64) - 127.0), 8, axis=1)[..., None]
    return vals.transpose(0, 1, 3, 2).reshape(g * 512, n)


E, I, O, N = 2, 2048, 2048, 256


def setup_inputs():
    s = mx_kscale(O)
    inputs = bf(np.random.standard_normal((E, O, N)) * s[None, :, None])
    stack = np.random.uniform(0.0, 1.0, (E, I, O)) * 1.7 / np.sqrt(O) / s[None, None, :]
    cat = np.ascontiguousarray(stack.swapaxes(1, 2)).reshape(-1, I)
    words, scales = pack_weight(cat, "e4m3")
    return {"inputs": inputs,
            "weight_words": words,
            "weight_scales": scales,
            "expert_size": E}


def reference(inputs, weight_words, weight_scales, expert_size):
    num_experts = E
    chunks = f64(inputs)[:num_experts]
    wq = unpack_weight(weight_words, weight_scales, "e4m3").reshape(E, O, I).swapaxes(1, 2)
    xq = mxq(chunks, 1, "e4m3")
    out = wq[None, :, :, :] @ xq[:, None, :, :]
    C = out.shape[0]
    return out.reshape(C * num_experts, I, inputs.shape[2])

@@ -1,0 +1,130 @@
+from contextlib import ExitStack
+
+import concourse.mybir as mybir
+
+BF16 = mybir.dt.bfloat16
+F32 = mybir.dt.float32
+I32 = mybir.dt.int32
+U32 = mybir.dt.uint32
+U8 = mybir.dt.uint8
+FP8X4 = mybir.dt.float8_e4m3fn_x4
+
+P = 128
+PACK = 4
+K_PASS = P * PACK
+
+EXPERTS = 2
+CHUNKS = 2
+K = 2048
+ROWS = 2048
+COLS = 256
+PASSES = K // K_PASS
+MOVING = CHUNKS * COLS
+BANKS = 8
+ROUND_ROWS = BANKS * P
+ROUNDS = ROWS // ROUND_ROWS
+QUADRANTS = 4
+RUN = 4
+
+FLOPS = 2 * CHUNKS * EXPERTS * ROWS * K * COLS
+
+
+def tile_flaxparallelexperts_e_kernel(tc, inputs, weight_words, weight_scales, expert_size, out):
+    nc = tc.nc
+
+    x_dram = inputs.rearrange("c (q p t) n -> q p c (t n)", p=P, t=PACK)
+    w_dram = weight_words.rearrange("g p n t -> g p (n t)")
+    out_dram = out.rearrange("(c e) (j p) n -> e j p c n", e=EXPERTS, p=P)
+
+    with ExitStack() as ctx:
+        ctx.enter_context(tc.manual_schedule())
+        keep = ctx.enter_context(tc.tile_pool(name="keep", bufs=1))
+        results = ctx.enter_context(tc.tile_pool(name="results", bufs=EXPERTS * ROUNDS * BANKS))
+        psum = ctx.enter_context(tc.psum_pool(name="psum", bufs=BANKS))
+
+        x_raw = [keep.tile([P, CHUNKS, PACK, COLS], BF16, name="x_raw%d" % q) for q in range(PASSES)]
+        x_grouped = [
+            keep.tile([P, MOVING, PACK], BF16, name="x_grouped%d" % q, align_bytes=64) for q in range(PASSES)
+        ]
+        x_words = [keep.tile([P, MOVING], U32, name="x_words%d" % q, align_bytes=64) for q in range(PASSES)]
+        x_scales = [keep.tile([P, MOVING], U8, name="x_scales%d" % q, align_bytes=64) for q in range(PASSES)]
+        w_words = [
+            [
+                [
+                    keep.tile([P, ROUND_ROWS], U32, name="w_words%d_%d_%d" % (e, q, r), align_bytes=64)
+                    for r in range(ROUNDS)
+                ]
+                for q in range(PASSES)
+            ]
+            for e in range(EXPERTS)
+        ]
+        w_scales = [keep.tile([P, ROWS], U8, name="w_scales%d" % e, align_bytes=64) for e in range(EXPERTS)]
+
+        def load_x(q):
+            nc.sync.dma_start(out=x_raw[q][:].rearrange("p c t n -> p c (t n)"), in_=x_dram[q])
+
+        def load_w_words(e, q, r):
+            byte_cols = slice(PACK * ROUND_ROWS * r, PACK * ROUND_ROWS * (r + 1))
+            nc.sync.dma_start(
+                out=w_words[e][q][r][:].bitcast(I32), in_=w_dram[PASSES * e + q][:, byte_cols].bitcast(I32)
+            )
+
+        def load_w_scales(e):
+            for quadrant in range(QUADRANTS):
+                first = 32 * quadrant
+                nc.sync.dma_start(
+                    out=w_scales[e][first : first + PASSES * 4, :].bitcast(I32),
+                    in_=weight_scales[
+                        PASSES * e : PASSES * (e + 1), 4 * quadrant : 4 * (quadrant + 1), :
+                    ].bitcast(I32),
+                )
+
+        def quantise_x(q):
+            for c, engine_copy in ((0, nc.vector.tensor_copy), (1, nc.scalar.copy)):
+                engine_copy(
+                    out=x_grouped[q][:, COLS * c : COLS * (c + 1), :].rearrange("p (b i) t -> p b t i", i=RUN),
+                    in_=x_raw[q][:, c, :, :].rearrange("p t (b i) -> p b t i", i=RUN),
+                )
+            nc.vector.quantize_mx(
+                out=x_words[q][:].bitcast(FP8X4),
+                scales=x_scales[q][:],
+                in_=x_grouped[q][:].rearrange("p w t -> p (w t)"),
+            )
+
+        for e in range(EXPERTS):
+            nc.vector.memset(w_scales[e][:].bitcast(I32), 0)
+
+        for q in range(PASSES):
+            load_x(q)
+            if q == 0:
+                load_w_scales(0)
+            load_w_words(0, q, 0)
+        for q in range(PASSES):
+            load_w_words(0, q, 1)
+        load_w_scales(1)
+        for r in range(ROUNDS):
+            for q in range(PASSES):
+                load_w_words(1, q, r)
+
+        for q in range(PASSES):
+            quantise_x(q)
+
+        for e in range(EXPERTS):
+            for r in range(ROUNDS):
+                accs = [psum.tile([P, MOVING], F32, name="acc%d" % b, tag="acc") for b in range(BANKS)]
+                for q in range(PASSES):
+                    for b in range(BANKS):
+                        nc.tensor.matmul_mx(
+                            out=accs[b][:],
+                            lhsT=w_words[e][q][r][:, P * b : P * (b + 1)].bitcast(FP8X4),
+                            lhsT_scale=w_scales[e][4 * q : P, ROUND_ROWS * r + P * b : ROUND_ROWS * r + P * (b + 1)],
+                            rhs=x_words[q][:].bitcast(FP8X4),
+                            rhs_scale=x_scales[q][:],
+                            start=(q == 0),
+                            stop=(q == PASSES - 1),
+                        )
+                for b in range(BANKS):
+                    result = results.tile([P, CHUNKS, COLS], F32)
+                    engine_copy = nc.vector.tensor_copy if b % 2 == 0 else nc.scalar.copy
+                    engine_copy(out=result[:].rearrange("p c n -> p (c n)"), in_=accs[b][:])
+                    nc.sync.dma_start(out=out_dram[e, BANKS * r + b], in_=result[:])

@@ -72,11 +72,11 @@ def tile_flaxparallelexperts_e_kernel(tc, inputs, weight_words, weight_scales, e
         def load_w_scales(e):
             for quadrant in range(QUADRANTS):
                 first = 32 * quadrant
-                nc.sync.dma_start(
-                    out=w_scales[e][first : first + PASSES * 4, :].bitcast(I32),
+                nc.gpsimd.dma_start(
+                    out=w_scales[e][first : first + PASSES * 4, :].bitcast(F32),
                     in_=weight_scales[
                         PASSES * e : PASSES * (e + 1), 4 * quadrant : 4 * (quadrant + 1), :
-                    ].bitcast(I32),
+                    ].bitcast(F32),
                 )
 
         def quantise_x(q):
@@ -94,14 +94,13 @@ def tile_flaxparallelexperts_e_kernel(tc, inputs, weight_words, weight_scales, e
         for e in range(EXPERTS):
             nc.vector.memset(w_scales[e][:].bitcast(I32), 0)
 
+        for e in range(EXPERTS):
+            load_w_scales(e)
         for q in range(PASSES):
             load_x(q)
-            if q == 0:
-                load_w_scales(0)
             load_w_words(0, q, 0)
         for q in range(PASSES):
             load_w_words(0, q, 1)
-        load_w_scales(1)
         for r in range(ROUNDS):
             for q in range(PASSES):
                 load_w_words(1, q, r)

@@ -49,13 +49,7 @@ def tile_flaxparallelexperts_e_kernel(tc, inputs, weight_words, weight_scales, e
         x_words = [keep.tile([P, MOVING], U32, name="x_words%d" % q, align_bytes=64) for q in range(PASSES)]
         x_scales = [keep.tile([P, MOVING], U8, name="x_scales%d" % q, align_bytes=64) for q in range(PASSES)]
         w_words = [
-            [
-                [
-                    keep.tile([P, ROUND_ROWS], U32, name="w_words%d_%d_%d" % (e, q, r), align_bytes=64)
-                    for r in range(ROUNDS)
-                ]
-                for q in range(PASSES)
-            ]
+            [keep.tile([P, ROWS], U32, name="w_words%d_%d" % (e, q), align_bytes=64) for q in range(PASSES)]
             for e in range(EXPERTS)
         ]
         w_scales = [keep.tile([P, ROWS], U8, name="w_scales%d" % e, align_bytes=64) for e in range(EXPERTS)]
@@ -63,20 +57,20 @@ def tile_flaxparallelexperts_e_kernel(tc, inputs, weight_words, weight_scales, e
         def load_x(q):
             nc.sync.dma_start(out=x_raw[q][:].rearrange("p c t n -> p c (t n)"), in_=x_dram[q])
 
-        def load_w_words(e, q, r):
-            byte_cols = slice(PACK * ROUND_ROWS * r, PACK * ROUND_ROWS * (r + 1))
+        def load_w_words(e, q, first_row, rows):
             nc.sync.dma_start(
-                out=w_words[e][q][r][:].bitcast(I32), in_=w_dram[PASSES * e + q][:, byte_cols].bitcast(I32)
+                out=w_words[e][q][:, first_row : first_row + rows].bitcast(I32),
+                in_=w_dram[PASSES * e + q][:, PACK * first_row : PACK * (first_row + rows)].bitcast(I32),
             )
 
-        def load_w_scales(e):
+        def load_w_scales(e, queue, view):
             for quadrant in range(QUADRANTS):
                 first = 32 * quadrant
-                nc.gpsimd.dma_start(
-                    out=w_scales[e][first : first + PASSES * 4, :].bitcast(F32),
+                queue.dma_start(
+                    out=w_scales[e][first : first + PASSES * 4, :].bitcast(view),
                     in_=weight_scales[
                         PASSES * e : PASSES * (e + 1), 4 * quadrant : 4 * (quadrant + 1), :
-                    ].bitcast(F32),
+                    ].bitcast(view),
                 )
 
         def quantise_x(q):
@@ -94,16 +88,16 @@ def tile_flaxparallelexperts_e_kernel(tc, inputs, weight_words, weight_scales, e
         for e in range(EXPERTS):
             nc.vector.memset(w_scales[e][:].bitcast(I32), 0)
 
-        for e in range(EXPERTS):
-            load_w_scales(e)
+        load_w_scales(1, nc.gpsimd, F32)
         for q in range(PASSES):
             load_x(q)
-            load_w_words(0, q, 0)
+            if q == 0:
+                load_w_scales(0, nc.sync, I32)
+            load_w_words(0, q, 0, ROUND_ROWS)
         for q in range(PASSES):
-            load_w_words(0, q, 1)
-        for r in range(ROUNDS):
-            for q in range(PASSES):
-                load_w_words(1, q, r)
+            load_w_words(0, q, ROUND_ROWS, ROUND_ROWS)
+        for q in range(PASSES):
+            load_w_words(1, q, 0, ROWS)
 
         for q in range(PASSES):
             quantise_x(q)
@@ -111,17 +105,21 @@ def tile_flaxparallelexperts_e_kernel(tc, inputs, weight_words, weight_scales, e
         for e in range(EXPERTS):
             for r in range(ROUNDS):
                 accs = [psum.tile([P, MOVING], F32, name="acc%d" % b, tag="acc") for b in range(BANKS)]
-                for q in range(PASSES):
-                    for b in range(BANKS):
-                        nc.tensor.matmul_mx(
-                            out=accs[b][:],
-                            lhsT=w_words[e][q][r][:, P * b : P * (b + 1)].bitcast(FP8X4),
-                            lhsT_scale=w_scales[e][4 * q : P, ROUND_ROWS * r + P * b : ROUND_ROWS * r + P * (b + 1)],
-                            rhs=x_words[q][:].bitcast(FP8X4),
-                            rhs_scale=x_scales[q][:],
-                            start=(q == 0),
-                            stop=(q == PASSES - 1),
-                        )
+                if e == 0 and r == 0:
+                    order = [(q, b) for q in range(PASSES) for b in range(BANKS)]
+                else:
+                    order = [(q, b) for b in range(BANKS) for q in range(PASSES)]
+                for q, b in order:
+                    rows = slice(ROUND_ROWS * r + P * b, ROUND_ROWS * r + P * (b + 1))
+                    nc.tensor.matmul_mx(
+                        out=accs[b][:],
+                        lhsT=w_words[e][q][:, rows].bitcast(FP8X4),
+                        lhsT_scale=w_scales[e][4 * q : P, rows],
+                        rhs=x_words[q][:].bitcast(FP8X4),
+                        rhs_scale=x_scales[q][:],
+                        start=(q == 0),
+                        stop=(q == PASSES - 1),
+                    )
                 for b in range(BANKS):
                     result = results.tile([P, CHUNKS, COLS], F32)
                     engine_copy = nc.vector.tensor_copy if b % 2 == 0 else nc.scalar.copy

@@ -33,7 +33,7 @@ def tile_flaxparallelexperts_e_kernel(tc, inputs, weight_words, weight_scales, e
     nc = tc.nc
 
     x_dram = inputs.rearrange("c (q p t) n -> q p c (t n)", p=P, t=PACK)
-    w_dram = weight_words.rearrange("g p n t -> g p (n t)")
+    w_dram = weight_words.rearrange("(e q) p n t -> e p q (n t)", e=EXPERTS)
     out_dram = out.rearrange("(c e) (j p) n -> e j p c n", e=EXPERTS, p=P)
 
     with ExitStack() as ctx:
@@ -48,19 +48,18 @@ def tile_flaxparallelexperts_e_kernel(tc, inputs, weight_words, weight_scales, e
         ]
         x_words = [keep.tile([P, MOVING], U32, name="x_words%d" % q, align_bytes=64) for q in range(PASSES)]
         x_scales = [keep.tile([P, MOVING], U8, name="x_scales%d" % q, align_bytes=64) for q in range(PASSES)]
-        w_words = [
-            [keep.tile([P, ROWS], U32, name="w_words%d_%d" % (e, q), align_bytes=64) for q in range(PASSES)]
-            for e in range(EXPERTS)
-        ]
+        w_words = [keep.tile([P, PASSES, ROWS], U32, name="w_words%d" % e, align_bytes=64) for e in range(EXPERTS)]
         w_scales = [keep.tile([P, ROWS], U8, name="w_scales%d" % e, align_bytes=64) for e in range(EXPERTS)]
 
         def load_x(q):
             nc.sync.dma_start(out=x_raw[q][:].rearrange("p c t n -> p c (t n)"), in_=x_dram[q])
 
-        def load_w_words(e, q, first_row, rows):
+        def load_w_words(e, first_q, passes, first_row, rows):
             nc.sync.dma_start(
-                out=w_words[e][q][:, first_row : first_row + rows].bitcast(I32),
-                in_=w_dram[PASSES * e + q][:, PACK * first_row : PACK * (first_row + rows)].bitcast(I32),
+                out=w_words[e][:, first_q : first_q + passes, first_row : first_row + rows].bitcast(I32),
+                in_=w_dram[e][
+                    :, first_q : first_q + passes, PACK * first_row : PACK * (first_row + rows)
+                ].bitcast(I32),
             )
 
         def load_w_scales(e, queue, view):
@@ -93,11 +92,11 @@ def tile_flaxparallelexperts_e_kernel(tc, inputs, weight_words, weight_scales, e
             load_x(q)
             if q == 0:
                 load_w_scales(0, nc.sync, I32)
-            load_w_words(0, q, 0, ROUND_ROWS)
-        for q in range(PASSES):
-            load_w_words(0, q, ROUND_ROWS, ROUND_ROWS)
-        for q in range(PASSES):
-            load_w_words(1, q, 0, ROWS)
+            load_w_words(0, q, 1, 0, ROUND_ROWS)
+        for first_tile, tiles in ((8, 2), (10, 2), (12, 4)):
+            load_w_words(0, 0, PASSES, P * first_tile, P * tiles)
+        for first_tile in range(0, ROWS // P, 4):
+            load_w_words(1, 0, PASSES, P * first_tile, P * 4)
 
         for q in range(PASSES):
             quantise_x(q)
@@ -113,7 +112,7 @@ def tile_flaxparallelexperts_e_kernel(tc, inputs, weight_words, weight_scales, e
                     rows = slice(ROUND_ROWS * r + P * b, ROUND_ROWS * r + P * (b + 1))
                     nc.tensor.matmul_mx(
                         out=accs[b][:],
-                        lhsT=w_words[e][q][:, rows].bitcast(FP8X4),
+                        lhsT=w_words[e][:, q, rows].bitcast(FP8X4),
                         lhsT_scale=w_scales[e][4 * q : P, rows],
                         rhs=x_words[q][:].bitcast(FP8X4),
                         rhs_scale=x_scales[q][:],

@@ -25,6 +25,11 @@ ROUND_ROWS = BANKS * P
 ROUNDS = ROWS // ROUND_ROWS
 QUADRANTS = 4
 RUN = 4
+TILES = ROWS // P
+GROUP = 4
+GROUP_ROWS = GROUP * P
+REGROUPED = ((0, 3), (1, 0), (1, 1), (1, 2))
+AHEAD = 4
 
 FLOPS = 2 * CHUNKS * EXPERTS * ROWS * K * COLS
 
@@ -35,11 +40,12 @@ def tile_flaxparallelexperts_e_kernel(tc, inputs, weight_words, weight_scales, e
     x_dram = inputs.rearrange("c (q p t) n -> q p c (t n)", p=P, t=PACK)
     w_dram = weight_words.rearrange("(e q) p n t -> e p q (n t)", e=EXPERTS)
     out_dram = out.rearrange("(c e) (j p) n -> e j p c n", e=EXPERTS, p=P)
+    out_group = out.rearrange("(c e) (g p a) n -> e g p c (a n)", e=EXPERTS, p=P, a=GROUP)
 
     with ExitStack() as ctx:
         ctx.enter_context(tc.manual_schedule())
         keep = ctx.enter_context(tc.tile_pool(name="keep", bufs=1))
-        results = ctx.enter_context(tc.tile_pool(name="results", bufs=EXPERTS * ROUNDS * BANKS))
+        results = ctx.enter_context(tc.tile_pool(name="results", bufs=EXPERTS * TILES - GROUP * len(REGROUPED)))
         psum = ctx.enter_context(tc.psum_pool(name="psum", bufs=BANKS))
 
         x_raw = [keep.tile([P, CHUNKS, PACK, COLS], BF16, name="x_raw%d" % q) for q in range(PASSES)]
@@ -50,6 +56,25 @@ def tile_flaxparallelexperts_e_kernel(tc, inputs, weight_words, weight_scales, e
         x_scales = [keep.tile([P, MOVING], U8, name="x_scales%d" % q, align_bytes=64) for q in range(PASSES)]
         w_words = [keep.tile([P, PASSES, ROWS], U32, name="w_words%d" % e, align_bytes=64) for e in range(EXPERTS)]
         w_scales = [keep.tile([P, ROWS], U8, name="w_scales%d" % e, align_bytes=64) for e in range(EXPERTS)]
+
+        w_regrouped = {}
+        s_regrouped = {}
+        group_result = {}
+        for key in REGROUPED:
+            w_regrouped[key] = keep.tile([P, PASSES, GROUP_ROWS], U32, name="w_regrouped%d_%d" % key, align_bytes=64)
+            s_regrouped[key] = keep.tile([P, GROUP_ROWS], U8, name="s_regrouped%d_%d" % key, align_bytes=64)
+            group_result[key] = keep.tile([P, CHUNKS, GROUP, COLS], F32, name="group_result%d_%d" % key)
+
+        def regroup(e, g):
+            cols = slice(GROUP_ROWS * g, GROUP_ROWS * (g + 1))
+            nc.vector.tensor_copy(
+                out=w_regrouped[(e, g)][:].bitcast(I32).rearrange("p q (a m) -> p q m a", a=GROUP),
+                in_=w_words[e][:, :, cols].bitcast(I32).rearrange("p q (m a) -> p q m a", a=GROUP),
+            )
+            nc.vector.tensor_copy(
+                out=s_regrouped[(e, g)][:].rearrange("p (a m) -> p m a", a=GROUP),
+                in_=w_scales[e][:, cols].rearrange("p (m a) -> p m a", a=GROUP),
+            )
 
         def load_x(q):
             nc.sync.dma_start(out=x_raw[q][:].rearrange("p c t n -> p c (t n)"), in_=x_dram[q])
@@ -101,26 +126,51 @@ def tile_flaxparallelexperts_e_kernel(tc, inputs, weight_words, weight_scales, e
         for q in range(PASSES):
             quantise_x(q)
 
-        for e in range(EXPERTS):
-            for r in range(ROUNDS):
-                accs = [psum.tile([P, MOVING], F32, name="acc%d" % b, tag="acc") for b in range(BANKS)]
-                if e == 0 and r == 0:
-                    order = [(q, b) for q in range(PASSES) for b in range(BANKS)]
-                else:
-                    order = [(q, b) for b in range(BANKS) for q in range(PASSES)]
-                for q, b in order:
-                    rows = slice(ROUND_ROWS * r + P * b, ROUND_ROWS * r + P * (b + 1))
-                    nc.tensor.matmul_mx(
-                        out=accs[b][:],
-                        lhsT=w_words[e][:, q, rows].bitcast(FP8X4),
-                        lhsT_scale=w_scales[e][4 * q : P, rows],
-                        rhs=x_words[q][:].bitcast(FP8X4),
-                        rhs_scale=x_scales[q][:],
-                        start=(q == 0),
-                        stop=(q == PASSES - 1),
+        def multiply(acc, e, j, q):
+            key = (e, j // GROUP)
+            if key in REGROUPED:
+                cols = slice(P * (j % GROUP), P * (j % GROUP + 1))
+                words, scales = w_regrouped[key][:, q, cols], s_regrouped[key][4 * q : P, cols]
+            else:
+                cols = slice(P * j, P * (j + 1))
+                words, scales = w_words[e][:, q, cols], w_scales[e][4 * q : P, cols]
+            nc.tensor.matmul_mx(
+                out=acc[:],
+                lhsT=words.bitcast(FP8X4),
+                lhsT_scale=scales,
+                rhs=x_words[q][:].bitcast(FP8X4),
+                rhs_scale=x_scales[q][:],
+                start=(q == 0),
+                stop=(q == PASSES - 1),
+            )
+
+        def empty(acc, e, j):
+            engine_copy = nc.vector.tensor_copy if j % 2 == 0 else nc.scalar.copy
+            key = (e, j // GROUP)
+            if key in REGROUPED:
+                engine_copy(
+                    out=group_result[key][:, :, j % GROUP, :], in_=acc[:].rearrange("p (c n) -> p c n", c=CHUNKS)
+                )
+                if j % GROUP == GROUP - 1:
+                    nc.sync.dma_start(
+                        out=out_group[e, j // GROUP], in_=group_result[key][:].rearrange("p c a n -> p c (a n)")
                     )
-                for b in range(BANKS):
-                    result = results.tile([P, CHUNKS, COLS], F32)
-                    engine_copy = nc.vector.tensor_copy if b % 2 == 0 else nc.scalar.copy
-                    engine_copy(out=result[:].rearrange("p c n -> p (c n)"), in_=accs[b][:])
-                    nc.sync.dma_start(out=out_dram[e, BANKS * r + b], in_=result[:])
+            else:
+                result = results.tile([P, CHUNKS, COLS], F32)
+                engine_copy(out=result[:].rearrange("p c n -> p (c n)"), in_=acc[:])
+                nc.sync.dma_start(out=out_dram[e, j], in_=result[:])
+
+        accs = [psum.tile([P, MOVING], F32, name="acc%d" % b, tag="acc") for b in range(BANKS)]
+        for q in range(PASSES):
+            for b in range(BANKS):
+                multiply(accs[b], 0, b, q)
+        for b in range(BANKS):
+            empty(accs[b], 0, b)
+        for t in range(BANKS, EXPERTS * TILES):
+            coming = ((t + AHEAD) // TILES, (t + AHEAD) % TILES // GROUP)
+            if (t + AHEAD) % GROUP == 0 and coming in REGROUPED:
+                regroup(coming[0], coming[1])
+            acc = psum.tile([P, MOVING], F32, name="acc", tag="acc")
+            for q in range(PASSES):
+                multiply(acc, t // TILES, t % TILES, q)
+            empty(acc, t // TILES, t % TILES)

@@ -28,7 +28,8 @@ RUN = 4
 TILES = ROWS // P
 GROUP = 4
 GROUP_ROWS = GROUP * P
-REGROUPED = ((0, 3), (1, 0), (1, 1), (1, 2))
+REGROUPED = ((1, 0), (1, 1), (1, 2))
+LATER_LOADS = ((0, 8, 2), (0, 10, 2), (0, 12, 4), (1, 0, 4), (1, 4, 4), (1, 8, 4), (1, 12, 4))
 AHEAD = 4
 
 FLOPS = 2 * CHUNKS * EXPERTS * ROWS * K * COLS
@@ -54,7 +55,12 @@ def tile_flaxparallelexperts_e_kernel(tc, inputs, weight_words, weight_scales, e
         ]
         x_words = [keep.tile([P, MOVING], U32, name="x_words%d" % q, align_bytes=64) for q in range(PASSES)]
         x_scales = [keep.tile([P, MOVING], U8, name="x_scales%d" % q, align_bytes=64) for q in range(PASSES)]
-        w_words = [keep.tile([P, PASSES, ROWS], U32, name="w_words%d" % e, align_bytes=64) for e in range(EXPERTS)]
+        w_first = [keep.tile([P, ROUND_ROWS], U32, name="w_first%d" % q, align_bytes=64) for q in range(PASSES)]
+        w_later = {}
+        for e, first_tile, tiles in LATER_LOADS:
+            loaded = keep.tile([P, PASSES, P * tiles], U32, name="w_later%d_%d" % (e, first_tile), align_bytes=64)
+            for j in range(first_tile, first_tile + tiles):
+                w_later[(e, j)] = (loaded, P * (j - first_tile))
         w_scales = [keep.tile([P, ROWS], U8, name="w_scales%d" % e, align_bytes=64) for e in range(EXPERTS)]
 
         w_regrouped = {}
@@ -68,23 +74,24 @@ def tile_flaxparallelexperts_e_kernel(tc, inputs, weight_words, weight_scales, e
         def regroup(e, g):
             cols = slice(GROUP_ROWS * g, GROUP_ROWS * (g + 1))
             nc.vector.tensor_copy(
-                out=w_regrouped[(e, g)][:].bitcast(I32).rearrange("p q (a m) -> p q m a", a=GROUP),
-                in_=w_words[e][:, :, cols].bitcast(I32).rearrange("p q (m a) -> p q m a", a=GROUP),
+                out=w_regrouped[(e, g)][:].bitcast(I32).rearrange("p q (a m) -> p q a m", a=GROUP),
+                in_=w_later[(e, GROUP * g)][0][:].bitcast(I32).rearrange("p q (m a) -> p q a m", a=GROUP),
             )
             nc.vector.tensor_copy(
-                out=s_regrouped[(e, g)][:].rearrange("p (a m) -> p m a", a=GROUP),
-                in_=w_scales[e][:, cols].rearrange("p (m a) -> p m a", a=GROUP),
+                out=s_regrouped[(e, g)][:].rearrange("p (a m) -> p a m", a=GROUP),
+                in_=w_scales[e][:, cols].rearrange("p (m a) -> p a m", a=GROUP),
             )
 
         def load_x(q):
             nc.sync.dma_start(out=x_raw[q][:].rearrange("p c t n -> p c (t n)"), in_=x_dram[q])
 
-        def load_w_words(e, first_q, passes, first_row, rows):
+        def load_w_first(q):
+            nc.sync.dma_start(out=w_first[q][:].bitcast(I32), in_=w_dram[0][:, q, 0 : PACK * ROUND_ROWS].bitcast(I32))
+
+        def load_w_later(e, first_tile, tiles):
             nc.sync.dma_start(
-                out=w_words[e][:, first_q : first_q + passes, first_row : first_row + rows].bitcast(I32),
-                in_=w_dram[e][
-                    :, first_q : first_q + passes, PACK * first_row : PACK * (first_row + rows)
-                ].bitcast(I32),
+                out=w_later[(e, first_tile)][0][:].bitcast(I32),
+                in_=w_dram[e][:, :, PACK * P * first_tile : PACK * P * (first_tile + tiles)].bitcast(I32),
             )
 
         def load_w_scales(e, queue, view):
@@ -117,11 +124,9 @@ def tile_flaxparallelexperts_e_kernel(tc, inputs, weight_words, weight_scales, e
             load_x(q)
             if q == 0:
                 load_w_scales(0, nc.sync, I32)
-            load_w_words(0, q, 1, 0, ROUND_ROWS)
-        for first_tile, tiles in ((8, 2), (10, 2), (12, 4)):
-            load_w_words(0, 0, PASSES, P * first_tile, P * tiles)
-        for first_tile in range(0, ROWS // P, 4):
-            load_w_words(1, 0, PASSES, P * first_tile, P * 4)
+            load_w_first(q)
+        for e, first_tile, tiles in LATER_LOADS:
+            load_w_later(e, first_tile, tiles)
 
         for q in range(PASSES):
             quantise_x(q)
@@ -133,7 +138,12 @@ def tile_flaxparallelexperts_e_kernel(tc, inputs, weight_words, weight_scales, e
                 words, scales = w_regrouped[key][:, q, cols], s_regrouped[key][4 * q : P, cols]
             else:
                 cols = slice(P * j, P * (j + 1))
-                words, scales = w_words[e][:, q, cols], w_scales[e][4 * q : P, cols]
+                scales = w_scales[e][4 * q : P, cols]
+                if (e, j) in w_later:
+                    loaded, first = w_later[(e, j)]
+                    words = loaded[:, q, first : first + P]
+                else:
+                    words = w_first[q][:, cols]
             nc.tensor.matmul_mx(
                 out=acc[:],
                 lhsT=words.bitcast(FP8X4),

@@ -30,6 +30,7 @@ GROUP = 4
 GROUP_ROWS = GROUP * P
 REGROUPED = ((1, 0), (1, 1), (1, 2))
 LATER_LOADS = ((0, 8, 2), (0, 10, 2), (0, 12, 4), (1, 0, 4), (1, 4, 4), (1, 8, 4), (1, 12, 4))
+WARM_UP = 12
 AHEAD = 4
 
 FLOPS = 2 * CHUNKS * EXPERTS * ROWS * K * COLS
@@ -49,7 +50,9 @@ def tile_flaxparallelexperts_e_kernel(tc, inputs, weight_words, weight_scales, e
         results = ctx.enter_context(tc.tile_pool(name="results", bufs=EXPERTS * TILES - GROUP * len(REGROUPED)))
         psum = ctx.enter_context(tc.psum_pool(name="psum", bufs=BANKS))
 
-        x_raw = [keep.tile([P, CHUNKS, PACK, COLS], BF16, name="x_raw%d" % q) for q in range(PASSES)]
+        x_raw = [
+            [keep.tile([P, PACK, COLS], BF16, name="x_raw%d_%d" % (q, c)) for c in range(CHUNKS)] for q in range(PASSES)
+        ]
         x_grouped = [
             keep.tile([P, MOVING, PACK], BF16, name="x_grouped%d" % q, align_bytes=64) for q in range(PASSES)
         ]
@@ -83,7 +86,8 @@ def tile_flaxparallelexperts_e_kernel(tc, inputs, weight_words, weight_scales, e
             )
 
         def load_x(q):
-            nc.sync.dma_start(out=x_raw[q][:].rearrange("p c t n -> p c (t n)"), in_=x_dram[q])
+            for c in range(CHUNKS):
+                nc.sync.dma_start(out=x_raw[q][c][:].rearrange("p t n -> p (t n)"), in_=x_dram[q][:, c, :])
 
         def load_w_first(q):
             nc.sync.dma_start(out=w_first[q][:].bitcast(I32), in_=w_dram[0][:, q, 0 : PACK * ROUND_ROWS].bitcast(I32))
@@ -105,10 +109,10 @@ def tile_flaxparallelexperts_e_kernel(tc, inputs, weight_words, weight_scales, e
                 )
 
         def quantise_x(q):
-            for c, engine_copy in ((0, nc.vector.tensor_copy), (1, nc.scalar.copy)):
+            for c, engine_copy in ((0, nc.scalar.copy), (1, nc.vector.tensor_copy)):
                 engine_copy(
                     out=x_grouped[q][:, COLS * c : COLS * (c + 1), :].rearrange("p (b i) t -> p b t i", i=RUN),
-                    in_=x_raw[q][:, c, :, :].rearrange("p t (b i) -> p b t i", i=RUN),
+                    in_=x_raw[q][c][:].rearrange("p t (b i) -> p b t i", i=RUN),
                 )
             nc.vector.quantize_mx(
                 out=x_words[q][:].bitcast(FP8X4),
@@ -118,6 +122,12 @@ def tile_flaxparallelexperts_e_kernel(tc, inputs, weight_words, weight_scales, e
 
         for e in range(EXPERTS):
             nc.vector.memset(w_scales[e][:].bitcast(I32), 0)
+
+        zeros = keep.tile([P, MOVING], BF16, name="zeros")
+        nc.vector.memset(zeros[:], 0.0)
+        warm = psum.tile([P, MOVING], F32, name="warm", tag="acc")
+        for i in range(WARM_UP):
+            nc.tensor.matmul(out=warm[:], lhsT=zeros[:, 0:P], rhs=zeros[:], start=True, stop=True)
 
         load_w_scales(1, nc.gpsimd, F32)
         for q in range(PASSES):
@@ -131,7 +141,7 @@ def tile_flaxparallelexperts_e_kernel(tc, inputs, weight_words, weight_scales, e
         for q in range(PASSES):
             quantise_x(q)
 
-        def multiply(acc, e, j, q):
+        def multiply(acc, e, j, q, moving=slice(0, MOVING)):
             key = (e, j // GROUP)
             if key in REGROUPED:
                 cols = slice(P * (j % GROUP), P * (j % GROUP + 1))
@@ -148,8 +158,8 @@ def tile_flaxparallelexperts_e_kernel(tc, inputs, weight_words, weight_scales, e
                 out=acc[:],
                 lhsT=words.bitcast(FP8X4),
                 lhsT_scale=scales,
-                rhs=x_words[q][:].bitcast(FP8X4),
-                rhs_scale=x_scales[q][:],
+                rhs=x_words[q][:, moving].bitcast(FP8X4),
+                rhs_scale=x_scales[q][:, moving],
                 start=(q == 0),
                 stop=(q == PASSES - 1),
             )
@@ -176,7 +186,7 @@ def tile_flaxparallelexperts_e_kernel(tc, inputs, weight_words, weight_scales, e
                 multiply(accs[b], 0, b, q)
         for b in range(BANKS):
             empty(accs[b], 0, b)
-        for t in range(BANKS, EXPERTS * TILES):
+        for t in range(BANKS, EXPERTS * TILES - 1):
             coming = ((t + AHEAD) // TILES, (t + AHEAD) % TILES // GROUP)
             if (t + AHEAD) % GROUP == 0 and coming in REGROUPED:
                 regroup(coming[0], coming[1])
@@ -184,3 +194,10 @@ def tile_flaxparallelexperts_e_kernel(tc, inputs, weight_words, weight_scales, e
             for q in range(PASSES):
                 multiply(acc, t // TILES, t % TILES, q)
             empty(acc, t // TILES, t % TILES)
+        for c, engine_copy in ((0, nc.vector.tensor_copy), (1, nc.scalar.copy)):
+            half = psum.tile([P, COLS], F32, name="half", tag="acc")
+            for q in range(PASSES):
+                multiply(half, EXPERTS - 1, TILES - 1, q, slice(COLS * c, COLS * (c + 1)))
+            half_result = keep.tile([P, COLS], F32, name="half_result%d" % c)
+            engine_copy(out=half_result[:], in_=half[:])
+            nc.sync.dma_start(out=out_dram[EXPERTS - 1, TILES - 1][:, c, :], in_=half_result[:])

@@ -28,9 +28,10 @@ RUN = 4
 TILES = ROWS // P
 GROUP = 4
 GROUP_ROWS = GROUP * P
-REGROUPED = ((1, 0), (1, 1), (1, 2))
+REGROUPED = ((0, 3), (1, 0), (1, 1), (1, 2))
 LATER_LOADS = ((0, 8, 2), (0, 10, 2), (0, 12, 4), (1, 0, 4), (1, 4, 4), (1, 8, 4), (1, 12, 4))
 WARM_UP = 12
+HEAD_TILES = 10
 AHEAD = 4
 
 FLOPS = 2 * CHUNKS * EXPERTS * ROWS * K * COLS
@@ -64,26 +65,41 @@ def tile_flaxparallelexperts_e_kernel(tc, inputs, weight_words, weight_scales, e
             loaded = keep.tile([P, PASSES, P * tiles], U32, name="w_later%d_%d" % (e, first_tile), align_bytes=64)
             for j in range(first_tile, first_tile + tiles):
                 w_later[(e, j)] = (loaded, P * (j - first_tile))
-        w_scales = [keep.tile([P, ROWS], U8, name="w_scales%d" % e, align_bytes=64) for e in range(EXPERTS)]
+        s_tiles = {
+            (0, 0): keep.tile([P, P * HEAD_TILES], U8, name="w_scales0_0", align_bytes=64),
+            (0, 1): keep.tile([P, ROWS - P * HEAD_TILES], U8, name="w_scales0_1", align_bytes=64),
+            (1, 0): keep.tile([P, ROWS], U8, name="w_scales1", align_bytes=64),
+        }
+
+        def scale_columns(e, first_row, rows):
+            if e == 0 and first_row < P * HEAD_TILES:
+                return s_tiles[(0, 0)], slice(first_row, first_row + rows)
+            if e == 0:
+                return s_tiles[(0, 1)], slice(first_row - P * HEAD_TILES, first_row - P * HEAD_TILES + rows)
+            return s_tiles[(1, 0)], slice(first_row, first_row + rows)
 
         w_regrouped = {}
         s_regrouped = {}
         group_result = {}
         for key in REGROUPED:
-            w_regrouped[key] = keep.tile([P, PASSES, GROUP_ROWS], U32, name="w_regrouped%d_%d" % key, align_bytes=64)
+            w_regrouped[key] = [
+                keep.tile([P, PASSES, P], U32, name="w_regrouped%d_%d_%d" % (key[0], key[1], a), align_bytes=64)
+                for a in range(GROUP)
+            ]
             s_regrouped[key] = keep.tile([P, GROUP_ROWS], U8, name="s_regrouped%d_%d" % key, align_bytes=64)
             group_result[key] = keep.tile([P, CHUNKS, GROUP, COLS], F32, name="group_result%d_%d" % key)
 
         def regroup(e, g):
-            cols = slice(GROUP_ROWS * g, GROUP_ROWS * (g + 1))
-            nc.vector.tensor_copy(
-                out=w_regrouped[(e, g)][:].bitcast(I32).rearrange("p q (a m) -> p q a m", a=GROUP),
-                in_=w_later[(e, GROUP * g)][0][:].bitcast(I32).rearrange("p q (m a) -> p q a m", a=GROUP),
-            )
+            plane, plane_cols = scale_columns(e, GROUP_ROWS * g, GROUP_ROWS)
             nc.vector.tensor_copy(
                 out=s_regrouped[(e, g)][:].rearrange("p (a m) -> p a m", a=GROUP),
-                in_=w_scales[e][:, cols].rearrange("p (m a) -> p a m", a=GROUP),
+                in_=plane[:, plane_cols].rearrange("p (m a) -> p a m", a=GROUP),
             )
+            for a in range(GROUP):
+                nc.vector.tensor_copy(
+                    out=w_regrouped[(e, g)][a][:].bitcast(I32),
+                    in_=w_later[(e, GROUP * g)][0][:].bitcast(I32).rearrange("p q (m a) -> p q a m", a=GROUP)[:, :, a, :],
+                )
 
         def load_x(q):
             for c in range(CHUNKS):
@@ -98,13 +114,14 @@ def tile_flaxparallelexperts_e_kernel(tc, inputs, weight_words, weight_scales, e
                 in_=w_dram[e][:, :, PACK * P * first_tile : PACK * P * (first_tile + tiles)].bitcast(I32),
             )
 
-        def load_w_scales(e, queue, view):
+        def load_w_scales(e, first_row, rows, queue, view):
+            plane, plane_cols = scale_columns(e, first_row, rows)
             for quadrant in range(QUADRANTS):
                 first = 32 * quadrant
                 queue.dma_start(
-                    out=w_scales[e][first : first + PASSES * 4, :].bitcast(view),
+                    out=plane[first : first + PASSES * 4, plane_cols].bitcast(view),
                     in_=weight_scales[
-                        PASSES * e : PASSES * (e + 1), 4 * quadrant : 4 * (quadrant + 1), :
+                        PASSES * e : PASSES * (e + 1), 4 * quadrant : 4 * (quadrant + 1), first_row : first_row + rows
                     ].bitcast(view),
                 )
 
@@ -120,8 +137,8 @@ def tile_flaxparallelexperts_e_kernel(tc, inputs, weight_words, weight_scales, e
                 in_=x_grouped[q][:].rearrange("p w t -> p (w t)"),
             )
 
-        for e in range(EXPERTS):
-            nc.vector.memset(w_scales[e][:].bitcast(I32), 0)
+        for key in ((0, 0), (1, 0), (0, 1)):
+            nc.vector.memset(s_tiles[key][:].bitcast(I32), 0)
 
         zeros = keep.tile([P, MOVING], BF16, name="zeros")
         nc.vector.memset(zeros[:], 0.0)
@@ -129,13 +146,15 @@ def tile_flaxparallelexperts_e_kernel(tc, inputs, weight_words, weight_scales, e
         for i in range(WARM_UP):
             nc.tensor.matmul(out=warm[:], lhsT=zeros[:, 0:P], rhs=zeros[:], start=True, stop=True)
 
-        load_w_scales(1, nc.gpsimd, F32)
+        load_w_scales(1, 0, ROWS, nc.gpsimd, F32)
         for q in range(PASSES):
             load_x(q)
             if q == 0:
-                load_w_scales(0, nc.sync, I32)
+                load_w_scales(0, 0, P * HEAD_TILES, nc.sync, I32)
             load_w_first(q)
         for e, first_tile, tiles in LATER_LOADS:
+            if (e, first_tile) == (0, HEAD_TILES):
+                load_w_scales(0, P * HEAD_TILES, ROWS - P * HEAD_TILES, nc.sync, I32)
             load_w_later(e, first_tile, tiles)
 
         for q in range(PASSES):
@@ -145,10 +164,11 @@ def tile_flaxparallelexperts_e_kernel(tc, inputs, weight_words, weight_scales, e
             key = (e, j // GROUP)
             if key in REGROUPED:
                 cols = slice(P * (j % GROUP), P * (j % GROUP + 1))
-                words, scales = w_regrouped[key][:, q, cols], s_regrouped[key][4 * q : P, cols]
+                words, scales = w_regrouped[key][j % GROUP][:, q, :], s_regrouped[key][4 * q : P, cols]
             else:
                 cols = slice(P * j, P * (j + 1))
-                scales = w_scales[e][4 * q : P, cols]
+                plane, plane_cols = scale_columns(e, P * j, P)
+                scales = plane[4 * q : P, plane_cols]
                 if (e, j) in w_later:
                     loaded, first = w_later[(e, j)]
                     words = loaded[:, q, first : first + P]

@@ -32,6 +32,7 @@ REGROUPED = ((0, 3), (1, 0), (1, 1), (1, 2))
 LATER_LOADS = ((0, 8, 2), (0, 10, 2), (0, 12, 4), (1, 0, 4), (1, 4, 4), (1, 8, 4), (1, 12, 4))
 WARM_UP = 12
 HEAD_TILES = 10
+SHIFT = 32
 AHEAD = 4
 
 FLOPS = 2 * CHUNKS * EXPERTS * ROWS * K * COLS
@@ -57,7 +58,8 @@ def tile_flaxparallelexperts_e_kernel(tc, inputs, weight_words, weight_scales, e
         x_grouped = [
             keep.tile([P, MOVING, PACK], BF16, name="x_grouped%d" % q, align_bytes=64) for q in range(PASSES)
         ]
-        x_words = [keep.tile([P, MOVING], U32, name="x_words%d" % q, align_bytes=64) for q in range(PASSES)]
+        x_padded = [keep.tile([P, 2 * SHIFT + MOVING], U32, name="x_words%d" % q, align_bytes=256) for q in range(PASSES)]
+        x_words = [x_padded[q][:, SHIFT : SHIFT + MOVING] for q in range(PASSES)]
         x_scales = [keep.tile([P, MOVING], U8, name="x_scales%d" % q, align_bytes=64) for q in range(PASSES)]
         w_first = [keep.tile([P, ROUND_ROWS], U32, name="w_first%d" % q, align_bytes=64) for q in range(PASSES)]
         w_later = {}
@@ -132,7 +134,7 @@ def tile_flaxparallelexperts_e_kernel(tc, inputs, weight_words, weight_scales, e
                     in_=x_raw[q][c][:].rearrange("p t (b i) -> p b t i", i=RUN),
                 )
             nc.vector.quantize_mx(
-                out=x_words[q][:].bitcast(FP8X4),
+                out=x_words[q].bitcast(FP8X4),
                 scales=x_scales[q][:],
                 in_=x_grouped[q][:].rearrange("p w t -> p (w t)"),
             )

from contextlib import ExitStack

import concourse.mybir as mybir

BF16 = mybir.dt.bfloat16
F32 = mybir.dt.float32
I32 = mybir.dt.int32
U32 = mybir.dt.uint32
U8 = mybir.dt.uint8
FP8X4 = mybir.dt.float8_e4m3fn_x4

P = 128
PACK = 4
K_PASS = P * PACK

EXPERTS = 2
CHUNKS = 2
K = 2048
ROWS = 2048
COLS = 256
PASSES = K // K_PASS
MOVING = CHUNKS * COLS
BANKS = 8
ROUND_ROWS = BANKS * P
ROUNDS = ROWS // ROUND_ROWS
QUADRANTS = 4
RUN = 4
TILES = ROWS // P
GROUP = 4
GROUP_ROWS = GROUP * P
REGROUPED = ((0, 3), (1, 0), (1, 1), (1, 2))
LATER_LOADS = ((0, 8, 2), (0, 10, 2), (0, 12, 4), (1, 0, 4), (1, 4, 4), (1, 8, 4), (1, 12, 4))
WARM_UP = 12
HEAD_TILES = 10
SHIFT = 32
AHEAD = 4

FLOPS = 2 * CHUNKS * EXPERTS * ROWS * K * COLS


def tile_flaxparallelexperts_e_kernel(tc, inputs, weight_words, weight_scales, expert_size, out):
    nc = tc.nc

    x_dram = inputs.rearrange("c (q p t) n -> q p c (t n)", p=P, t=PACK)
    w_dram = weight_words.rearrange("(e q) p n t -> e p q (n t)", e=EXPERTS)
    out_dram = out.rearrange("(c e) (j p) n -> e j p c n", e=EXPERTS, p=P)
    out_group = out.rearrange("(c e) (g p a) n -> e g p c (a n)", e=EXPERTS, p=P, a=GROUP)

    with ExitStack() as ctx:
        ctx.enter_context(tc.manual_schedule())
        keep = ctx.enter_context(tc.tile_pool(name="keep", bufs=1))
        results = ctx.enter_context(tc.tile_pool(name="results", bufs=EXPERTS * TILES - GROUP * len(REGROUPED)))
        psum = ctx.enter_context(tc.psum_pool(name="psum", bufs=BANKS))

        x_raw = [
            [keep.tile([P, PACK, COLS], BF16, name="x_raw%d_%d" % (q, c)) for c in range(CHUNKS)] for q in range(PASSES)
        ]
        x_grouped = [
            keep.tile([P, MOVING, PACK], BF16, name="x_grouped%d" % q, align_bytes=64) for q in range(PASSES)
        ]
        x_padded = [keep.tile([P, 2 * SHIFT + MOVING], U32, name="x_words%d" % q, align_bytes=256) for q in range(PASSES)]
        x_words = [x_padded[q][:, SHIFT : SHIFT + MOVING] for q in range(PASSES)]
        x_scales = [keep.tile([P, MOVING], U8, name="x_scales%d" % q, align_bytes=64) for q in range(PASSES)]
        w_first = [keep.tile([P, ROUND_ROWS], U32, name="w_first%d" % q, align_bytes=64) for q in range(PASSES)]
        w_later = {}
        for e, first_tile, tiles in LATER_LOADS:
            loaded = keep.tile([P, PASSES, P * tiles], U32, name="w_later%d_%d" % (e, first_tile), align_bytes=64)
            for j in range(first_tile, first_tile + tiles):
                w_later[(e, j)] = (loaded, P * (j - first_tile))
        s_tiles = {
            (0, 0): keep.tile([P, P * HEAD_TILES], U8, name="w_scales0_0", align_bytes=64),
            (0, 1): keep.tile([P, ROWS - P * HEAD_TILES], U8, name="w_scales0_1", align_bytes=64),
            (1, 0): keep.tile([P, ROWS], U8, name="w_scales1", align_bytes=64),
        }

        def scale_columns(e, first_row, rows):
            if e == 0 and first_row < P * HEAD_TILES:
                return s_tiles[(0, 0)], slice(first_row, first_row + rows)
            if e == 0:
                return s_tiles[(0, 1)], slice(first_row - P * HEAD_TILES, first_row - P * HEAD_TILES + rows)
            return s_tiles[(1, 0)], slice(first_row, first_row + rows)

        w_regrouped = {}
        s_regrouped = {}
        group_result = {}
        for key in REGROUPED:
            w_regrouped[key] = [
                keep.tile([P, PASSES, P], U32, name="w_regrouped%d_%d_%d" % (key[0], key[1], a), align_bytes=64)
                for a in range(GROUP)
            ]
            s_regrouped[key] = keep.tile([P, GROUP_ROWS], U8, name="s_regrouped%d_%d" % key, align_bytes=64)
            group_result[key] = keep.tile([P, CHUNKS, GROUP, COLS], F32, name="group_result%d_%d" % key)

        def regroup(e, g):
            plane, plane_cols = scale_columns(e, GROUP_ROWS * g, GROUP_ROWS)
            nc.vector.tensor_copy(
                out=s_regrouped[(e, g)][:].rearrange("p (a m) -> p a m", a=GROUP),
                in_=plane[:, plane_cols].rearrange("p (m a) -> p a m", a=GROUP),
            )
            for a in range(GROUP):
                nc.vector.tensor_copy(
                    out=w_regrouped[(e, g)][a][:].bitcast(I32),
                    in_=w_later[(e, GROUP * g)][0][:].bitcast(I32).rearrange("p q (m a) -> p q a m", a=GROUP)[:, :, a, :],
                )

        def load_x(q):
            for c in range(CHUNKS):
                nc.sync.dma_start(out=x_raw[q][c][:].rearrange("p t n -> p (t n)"), in_=x_dram[q][:, c, :])

        def load_w_first(q):
            nc.sync.dma_start(out=w_first[q][:].bitcast(I32), in_=w_dram[0][:, q, 0 : PACK * ROUND_ROWS].bitcast(I32))

        def load_w_later(e, first_tile, tiles):
            nc.sync.dma_start(
                out=w_later[(e, first_tile)][0][:].bitcast(I32),
                in_=w_dram[e][:, :, PACK * P * first_tile : PACK * P * (first_tile + tiles)].bitcast(I32),
            )

        def load_w_scales(e, first_row, rows, queue, view):
            plane, plane_cols = scale_columns(e, first_row, rows)
            for quadrant in range(QUADRANTS):
                first = 32 * quadrant
                queue.dma_start(
                    out=plane[first : first + PASSES * 4, plane_cols].bitcast(view),
                    in_=weight_scales[
                        PASSES * e : PASSES * (e + 1), 4 * quadrant : 4 * (quadrant + 1), first_row : first_row + rows
                    ].bitcast(view),
                )

        def quantise_x(q):
            for c, engine_copy in ((0, nc.scalar.copy), (1, nc.vector.tensor_copy)):
                engine_copy(
                    out=x_grouped[q][:, COLS * c : COLS * (c + 1), :].rearrange("p (b i) t -> p b t i", i=RUN),
                    in_=x_raw[q][c][:].rearrange("p t (b i) -> p b t i", i=RUN),
                )
            nc.vector.quantize_mx(
                out=x_words[q].bitcast(FP8X4),
                scales=x_scales[q][:],
                in_=x_grouped[q][:].rearrange("p w t -> p (w t)"),
            )

        for key in ((0, 0), (1, 0), (0, 1)):
            nc.vector.memset(s_tiles[key][:].bitcast(I32), 0)

        zeros = keep.tile([P, MOVING], BF16, name="zeros")
        nc.vector.memset(zeros[:], 0.0)
        warm = psum.tile([P, MOVING], F32, name="warm", tag="acc")
        for i in range(WARM_UP):
            nc.tensor.matmul(out=warm[:], lhsT=zeros[:, 0:P], rhs=zeros[:], start=True, stop=True)

        load_w_scales(1, 0, ROWS, nc.gpsimd, F32)
        for q in range(PASSES):
            load_x(q)
            if q == 0:
                load_w_scales(0, 0, P * HEAD_TILES, nc.sync, I32)
            load_w_first(q)
        for e, first_tile, tiles in LATER_LOADS:
            if (e, first_tile) == (0, HEAD_TILES):
                load_w_scales(0, P * HEAD_TILES, ROWS - P * HEAD_TILES, nc.sync, I32)
            load_w_later(e, first_tile, tiles)

        for q in range(PASSES):
            quantise_x(q)

        def multiply(acc, e, j, q, moving=slice(0, MOVING)):
            key = (e, j // GROUP)
            if key in REGROUPED:
                cols = slice(P * (j % GROUP), P * (j % GROUP + 1))
                words, scales = w_regrouped[key][j % GROUP][:, q, :], s_regrouped[key][4 * q : P, cols]
            else:
                cols = slice(P * j, P * (j + 1))
                plane, plane_cols = scale_columns(e, P * j, P)
                scales = plane[4 * q : P, plane_cols]
                if (e, j) in w_later:
                    loaded, first = w_later[(e, j)]
                    words = loaded[:, q, first : first + P]
                else:
                    words = w_first[q][:, cols]
            nc.tensor.matmul_mx(
                out=acc[:],
                lhsT=words.bitcast(FP8X4),
                lhsT_scale=scales,
                rhs=x_words[q][:, moving].bitcast(FP8X4),
                rhs_scale=x_scales[q][:, moving],
                start=(q == 0),
                stop=(q == PASSES - 1),
            )

        def empty(acc, e, j):
            engine_copy = nc.vector.tensor_copy if j % 2 == 0 else nc.scalar.copy
            key = (e, j // GROUP)
            if key in REGROUPED:
                engine_copy(
                    out=group_result[key][:, :, j % GROUP, :], in_=acc[:].rearrange("p (c n) -> p c n", c=CHUNKS)
                )
                if j % GROUP == GROUP - 1:
                    nc.sync.dma_start(
                        out=out_group[e, j // GROUP], in_=group_result[key][:].rearrange("p c a n -> p c (a n)")
                    )
            else:
                result = results.tile([P, CHUNKS, COLS], F32)
                engine_copy(out=result[:].rearrange("p c n -> p (c n)"), in_=acc[:])
                nc.sync.dma_start(out=out_dram[e, j], in_=result[:])

        accs = [psum.tile([P, MOVING], F32, name="acc%d" % b, tag="acc") for b in range(BANKS)]
        for q in range(PASSES):
            for b in range(BANKS):
                multiply(accs[b], 0, b, q)
        for b in range(BANKS):
            empty(accs[b], 0, b)
        for t in range(BANKS, EXPERTS * TILES - 1):
            coming = ((t + AHEAD) // TILES, (t + AHEAD) % TILES // GROUP)
            if (t + AHEAD) % GROUP == 0 and coming in REGROUPED:
                regroup(coming[0], coming[1])
            acc = psum.tile([P, MOVING], F32, name="acc", tag="acc")
            for q in range(PASSES):
                multiply(acc, t // TILES, t % TILES, q)
            empty(acc, t // TILES, t % TILES)
        for c, engine_copy in ((0, nc.vector.tensor_copy), (1, nc.scalar.copy)):
            half = psum.tile([P, COLS], F32, name="half", tag="acc")
            for q in range(PASSES):
                multiply(half, EXPERTS - 1, TILES - 1, q, slice(COLS * c, COLS * (c + 1)))
            half_result = keep.tile([P, COLS], F32, name="half_result%d" % c)
            engine_copy(out=half_result[:], in_=half[:])
            nc.sync.dma_start(out=out_dram[EXPERTS - 1, TILES - 1][:, c, :], in_=half_result[:])
